import numpy as np
import ml_dtypes


def mxq(x, axis, fmt="e4m3"):
    dtype, down = {"e4m3": (ml_dtypes.float8_e4m3fn, 7), "e5m2": (ml_dtypes.float8_e5m2, 14)}[fmt]
    v = np.moveaxis(np.asarray(x, np.float32).astype(ml_dtypes.bfloat16).astype(np.float64), axis, -1)
    blocks = v.reshape(v.shape[:-1] + (-1, 32))
    amax = np.abs(blocks).max(-1, keepdims=True)
    byte = np.maximum(np.where(amax > 0, np.frexp(amax)[1] - 1 + 127, 0) - down, 1)
    scale = np.exp2(byte - 127.0)
    codes = (blocks / scale).astype(np.float32).astype(dtype).astype(np.float64)
    return np.moveaxis((codes * scale).reshape(v.shape), -1, axis)


WIDE = False


def mx_kscale(k):
    if not WIDE:
        return np.ones(k)
    levels = np.array([10, -10, 5, -5, 0])
    a = np.random.permutation(np.resize(levels, k // 512 * 4)).reshape(k // 512, 4)
    idx = np.arange(k)
    return np.exp2(a[idx // 512, idx % 128 // 32])


BF16 = ml_dtypes.bfloat16


def bf(x):
    return np.asarray(x, np.float32).astype(BF16)


def f64(x):
    return np.asarray(x).astype(np.float64)


N, C, T, V, H, QK = 8, 128, 128, 64, 4, 16
K = QK * V
MQ = np.sqrt(0.5 * np.sqrt(QK))


def setup_inputs():
    s = mx_kscale(K).reshape(QK, 1, V)
    q = MQ * np.random.standard_normal((N, H, QK, T, 1)) + 1.6 * np.random.standard_normal((N, H, QK, T, V))
    k = MQ * np.random.standard_normal((N, H, QK, T, 1)) + 1.6 * np.random.standard_normal((N, H, QK, T, V))
    return {"q": bf(q * s), "k": bf(k / s),
            "alphas": bf(0.2 * (1.0 + 0.3 * np.random.standard_normal((1, H, 1, 1)))),
            "att1s": bf(np.eye(T)[None, None] + 0.05 * np.random.standard_normal((1, H, T, T)))}


def reference(q, k, alphas, att1s):
    qf = np.swapaxes(f64(q), 2, 3).reshape(N, H, T, K)
    kf = np.swapaxes(f64(k), 2, 3).reshape(N, H, T, K)
    sc = mxq(qf, 3, "e4m3") @ np.swapaxes(mxq(kf, 3, "e4m3"), 2, 3)
    return np.tanh(sc / (QK * V)) * f64(alphas) + f64(att1s)

@@ -1,0 +1,128 @@
+from contextlib import ExitStack
+
+import concourse.mybir as mybir
+from concourse.masks import make_identity
+
+F32 = mybir.dt.float32
+BF16 = mybir.dt.bfloat16
+U32 = mybir.dt.uint32
+U8 = mybir.dt.uint8
+FP8X4 = mybir.dt.float8_e4m3fn_x4
+
+SAMPLES, HEADS, CHANNELS, FRAMES, JOINTS = 8, 4, 16, 128, 64
+FLOPS = 2 * SAMPLES * HEADS * FRAMES * FRAMES * CHANNELS * JOINTS
+
+P = 128
+PASSES = CHANNELS * JOINTS // (4 * P)
+GROUP = 4
+FRAMES_LOW = 8
+FRAMES_HIGH = FRAMES // FRAMES_LOW
+RUN = FRAMES_LOW * JOINTS
+WIDTH = PASSES * GROUP * RUN
+
+
+def load(nc, pool, x, head, first_sample, name):
+    raw = pool.tile([P, PASSES, GROUP, RUN], BF16, name=name, align_bytes=64)
+    runs = x.rearrange(
+        "n h (a b g) (y l) v -> h a b (g y) n (l v)", a=PASSES, b=2, g=4, l=FRAMES_LOW
+    )
+    for a in range(PASSES):
+        for b in range(2):
+            nc.sync.dma_start(
+                out=raw[b:P:2, a, :, :],
+                in_=runs[head, a, b, :, first_sample : first_sample + GROUP, :],
+            )
+    return raw
+
+
+def turn_and_quantise(nc, turned_pool, mx_pool, raw):
+    turned = turned_pool.tile([P, WIDTH], BF16, align_bytes=64)
+    nc.vector.transpose(
+        out=turned[:].bitcast(F32),
+        in_=raw[:].rearrange("p a n e -> p (a n e)").bitcast(F32),
+    )
+    codes = mx_pool.tile([P, PASSES, GROUP, FRAMES], U32, align_bytes=64)
+    scales = mx_pool.tile([P, PASSES, GROUP, FRAMES], U8, align_bytes=64)
+    nc.vector.quantize_mx(
+        out=codes[:].rearrange("p a n f -> p (a n f)").bitcast(FP8X4),
+        scales=scales[:].rearrange("p a n f -> p (a n f)"),
+        in_=turned[:],
+    )
+    return codes, scales
+
+
+def tile_model_pa_t_kernel(tc, q, k, alphas, att1s, out):
+    nc = tc.nc
+    rounds = [(head, first) for head in range(HEADS) for first in range(0, SAMPLES, GROUP)]
+
+    with ExitStack() as stack:
+        const = stack.enter_context(tc.tile_pool(name="const", bufs=1))
+        raw_pool = stack.enter_context(tc.tile_pool(name="raw", bufs=len(rounds)))
+        turned_pool = stack.enter_context(tc.tile_pool(name="turned", bufs=3))
+        mx_pool = stack.enter_context(tc.tile_pool(name="mx", bufs=4))
+        out_pool = stack.enter_context(tc.tile_pool(name="outs", bufs=2))
+        psum = stack.enter_context(tc.psum_pool(name="psum", bufs=2))
+
+        raws = [
+            (load(nc, raw_pool, q, head, first, "q_raw"), load(nc, raw_pool, k, head, first, "k_raw"))
+            for head, first in rounds
+        ]
+
+        static_map = const.tile([P, HEADS, FRAMES], BF16)
+        nc.scalar.dma_start(out=static_map[:], in_=att1s[0].rearrange("h t u -> t h u"))
+        gain_bf = const.tile([P, HEADS], BF16)
+        nc.scalar.dma_start(
+            out=gain_bf[:], in_=alphas.rearrange("a h b c -> (a h b c)").partition_broadcast(P)
+        )
+        gain = const.tile([P, HEADS], F32)
+        nc.vector.tensor_copy(out=gain[:], in_=gain_bf[:])
+
+        identity = const.tile([P, P], F32)
+        make_identity(nc, identity[:])
+        sort_frames = const.tile([P, P], F32)
+        nc.vector.tensor_copy(
+            out=sort_frames[:].rearrange("p (y l) -> p y l", l=FRAMES_LOW),
+            in_=identity[:].rearrange("p (l y) -> p y l", l=FRAMES_LOW),
+        )
+
+        for (head, first), (q_raw, k_raw) in zip(rounds, raws):
+            q_codes, q_scales = turn_and_quantise(nc, turned_pool, mx_pool, q_raw)
+            k_codes, k_scales = turn_and_quantise(nc, turned_pool, mx_pool, k_raw)
+
+            scores = psum.tile([P, GROUP, FRAMES], F32)
+            for n in range(GROUP):
+                for a in range(PASSES):
+                    nc.tensor.matmul_mx(
+                        out=scores[:, n, :],
+                        lhsT=k_codes[:, a, n, :].bitcast(FP8X4),
+                        lhsT_scale=k_scales[:, a, n, :],
+                        rhs=q_codes[:, a, n, :].bitcast(FP8X4),
+                        rhs_scale=q_scales[:, a, n, :],
+                        start=(a == 0),
+                        stop=(a == PASSES - 1),
+                    )
+
+            squashed = out_pool.tile([P, GROUP, FRAMES], F32)
+            nc.scalar.activation(
+                out=squashed[:].rearrange("p n (y l) -> p n y l", l=FRAMES_LOW),
+                in_=scores[:].rearrange("p n (l y) -> p n y l", l=FRAMES_LOW),
+                func=mybir.ActivationFunctionType.Tanh,
+                scale=1.0 / (CHANNELS * JOINTS),
+            )
+
+            by_frame = psum.tile([P, GROUP, FRAMES], F32)
+            for n in range(GROUP):
+                nc.tensor.transpose(by_frame[:, n, :], squashed[:, n, :], sort_frames[:])
+
+            result = out_pool.tile([P, GROUP, FRAMES], F32)
+            nc.vector.scalar_tensor_tensor(
+                out=result[:],
+                in0=by_frame[:],
+                scalar=gain[:, head : head + 1],
+                in1=static_map[:, head, :].unsqueeze(1).to_broadcast([P, GROUP, FRAMES]),
+                op0=mybir.AluOpType.mult,
+                op1=mybir.AluOpType.add,
+            )
+            nc.scalar.dma_start(
+                out=out[first : first + GROUP, head].rearrange("n t u -> t n u"), in_=result[:]
+            )

@@ -35,14 +35,18 @@ def load(nc, pool, x, head, first_sample, name):
     return raw
 
 
-def turn_and_quantise(nc, turned_pool, mx_pool, raw):
-    turned = turned_pool.tile([P, WIDTH], BF16, align_bytes=64)
+def turn(nc, pool, raw):
+    turned = pool.tile([P, WIDTH], BF16, align_bytes=64)
     nc.vector.transpose(
         out=turned[:].bitcast(F32),
         in_=raw[:].rearrange("p a n e -> p (a n e)").bitcast(F32),
     )
-    codes = mx_pool.tile([P, PASSES, GROUP, FRAMES], U32, align_bytes=64)
-    scales = mx_pool.tile([P, PASSES, GROUP, FRAMES], U8, align_bytes=64)
+    return turned
+
+
+def quantise(nc, pool, turned):
+    codes = pool.tile([P, PASSES, GROUP, FRAMES], U32, align_bytes=64)
+    scales = pool.tile([P, PASSES, GROUP, FRAMES], U8, align_bytes=64)
     nc.vector.quantize_mx(
         out=codes[:].rearrange("p a n f -> p (a n f)").bitcast(FP8X4),
         scales=scales[:].rearrange("p a n f -> p (a n f)"),
@@ -85,9 +89,29 @@ def tile_model_pa_t_kernel(tc, q, k, alphas, att1s, out):
             in_=identity[:].rearrange("p (l y) -> p y l", l=FRAMES_LOW),
         )
 
+        def finish(head, first, by_frame):
+            result = out_pool.tile([P, GROUP, FRAMES], F32)
+            nc.vector.scalar_tensor_tensor(
+                out=result[:],
+                in0=by_frame[:],
+                scalar=gain[:, head : head + 1],
+                in1=static_map[:, head, :].unsqueeze(1).to_broadcast([P, GROUP, FRAMES]),
+                op0=mybir.AluOpType.mult,
+                op1=mybir.AluOpType.add,
+            )
+            nc.scalar.dma_start(
+                out=out[first : first + GROUP, head].rearrange("n t u -> t n u"), in_=result[:]
+            )
+
+        stack.enter_context(tc.manual_schedule())
+        waiting = None
         for (head, first), (q_raw, k_raw) in zip(rounds, raws):
-            q_codes, q_scales = turn_and_quantise(nc, turned_pool, mx_pool, q_raw)
-            k_codes, k_scales = turn_and_quantise(nc, turned_pool, mx_pool, k_raw)
+            q_turned = turn(nc, turned_pool, q_raw)
+            k_turned = turn(nc, turned_pool, k_raw)
+            if waiting is not None:
+                finish(*waiting)
+            q_codes, q_scales = quantise(nc, mx_pool, q_turned)
+            k_codes, k_scales = quantise(nc, mx_pool, k_turned)
 
             scores = psum.tile([P, GROUP, FRAMES], F32)
             for n in range(GROUP):
@@ -113,16 +137,5 @@ def tile_model_pa_t_kernel(tc, q, k, alphas, att1s, out):
             by_frame = psum.tile([P, GROUP, FRAMES], F32)
             for n in range(GROUP):
                 nc.tensor.transpose(by_frame[:, n, :], squashed[:, n, :], sort_frames[:])
-
-            result = out_pool.tile([P, GROUP, FRAMES], F32)
-            nc.vector.scalar_tensor_tensor(
-                out=result[:],
-                in0=by_frame[:],
-                scalar=gain[:, head : head + 1],
-                in1=static_map[:, head, :].unsqueeze(1).to_broadcast([P, GROUP, FRAMES]),
-                op0=mybir.AluOpType.mult,
-                op1=mybir.AluOpType.add,
-            )
-            nc.scalar.dma_start(
-                out=out[first : first + GROUP, head].rearrange("n t u -> t n u"), in_=result[:]
-            )
+            waiting = (head, first, by_frame)
+        finish(*waiting)

@@ -19,6 +19,8 @@ FRAMES_LOW = 8
 FRAMES_HIGH = FRAMES // FRAMES_LOW
 RUN = FRAMES_LOW * JOINTS
 WIDTH = PASSES * GROUP * RUN
+PSUM_BANKS = 8
+LAG = 6
 
 
 def load(nc, pool, x, head, first_sample, name):
@@ -64,8 +66,10 @@ def tile_model_pa_t_kernel(tc, q, k, alphas, att1s, out):
         raw_pool = stack.enter_context(tc.tile_pool(name="raw", bufs=len(rounds)))
         turned_pool = stack.enter_context(tc.tile_pool(name="turned", bufs=3))
         mx_pool = stack.enter_context(tc.tile_pool(name="mx", bufs=4))
-        out_pool = stack.enter_context(tc.tile_pool(name="outs", bufs=2))
-        psum = stack.enter_context(tc.psum_pool(name="psum", bufs=2))
+        squashed_pool = stack.enter_context(tc.tile_pool(name="squashed", bufs=2))
+        result_pool = stack.enter_context(tc.tile_pool(name="result", bufs=LAG))
+        scores_pool = stack.enter_context(tc.psum_pool(name="scores", bufs=PSUM_BANKS - LAG))
+        by_frame_pool = stack.enter_context(tc.psum_pool(name="by_frame", bufs=LAG))
 
         raws = [
             (load(nc, raw_pool, q, head, first, "q_raw"), load(nc, raw_pool, k, head, first, "k_raw"))
@@ -90,7 +94,7 @@ def tile_model_pa_t_kernel(tc, q, k, alphas, att1s, out):
         )
 
         def finish(head, first, by_frame):
-            result = out_pool.tile([P, GROUP, FRAMES], F32)
+            result = result_pool.tile([P, GROUP, FRAMES], F32)
             nc.vector.scalar_tensor_tensor(
                 out=result[:],
                 in0=by_frame[:],
@@ -104,16 +108,16 @@ def tile_model_pa_t_kernel(tc, q, k, alphas, att1s, out):
             )
 
         stack.enter_context(tc.manual_schedule())
-        waiting = None
-        for (head, first), (q_raw, k_raw) in zip(rounds, raws):
+        waiting = []
+        for r, ((head, first), (q_raw, k_raw)) in enumerate(zip(rounds, raws)):
             q_turned = turn(nc, turned_pool, q_raw)
             k_turned = turn(nc, turned_pool, k_raw)
-            if waiting is not None:
-                finish(*waiting)
+            if r >= LAG:
+                finish(*waiting[r - LAG])
             q_codes, q_scales = quantise(nc, mx_pool, q_turned)
             k_codes, k_scales = quantise(nc, mx_pool, k_turned)
 
-            scores = psum.tile([P, GROUP, FRAMES], F32)
+            scores = scores_pool.tile([P, GROUP, FRAMES], F32)
             for n in range(GROUP):
                 for a in range(PASSES):
                     nc.tensor.matmul_mx(
@@ -126,7 +130,7 @@ def tile_model_pa_t_kernel(tc, q, k, alphas, att1s, out):
                         stop=(a == PASSES - 1),
                     )
 
-            squashed = out_pool.tile([P, GROUP, FRAMES], F32)
+            squashed = squashed_pool.tile([P, GROUP, FRAMES], F32)
             nc.scalar.activation(
                 out=squashed[:].rearrange("p n (y l) -> p n y l", l=FRAMES_LOW),
                 in_=scores[:].rearrange("p n (l y) -> p n y l", l=FRAMES_LOW),
@@ -134,8 +138,9 @@ def tile_model_pa_t_kernel(tc, q, k, alphas, att1s, out):
                 scale=1.0 / (CHANNELS * JOINTS),
             )
 
-            by_frame = psum.tile([P, GROUP, FRAMES], F32)
+            by_frame = by_frame_pool.tile([P, GROUP, FRAMES], F32)
             for n in range(GROUP):
                 nc.tensor.transpose(by_frame[:, n, :], squashed[:, n, :], sort_frames[:])
-            waiting = (head, first, by_frame)
-        finish(*waiting)
+            waiting.append((head, first, by_frame))
+        for late in waiting[len(rounds) - LAG :]:
+            finish(*late)

@@ -16,45 +16,38 @@ P = 128
 PASSES = CHANNELS * JOINTS // (4 * P)
 GROUP = 4
 FRAMES_LOW = 8
-FRAMES_HIGH = FRAMES // FRAMES_LOW
 RUN = FRAMES_LOW * JOINTS
-WIDTH = PASSES * GROUP * RUN
 PSUM_BANKS = 8
-LAG = 6
+LAG = 7
 
 
-def load(nc, pool, x, head, first_sample, name):
-    raw = pool.tile([P, PASSES, GROUP, RUN], BF16, name=name, align_bytes=64)
+def load(nc, pool, x, head, first_sample, a, name):
+    raw = pool.tile([P, GROUP, RUN], BF16, name=name, align_bytes=64)
     runs = x.rearrange(
         "n h (a b g) (y l) v -> h a b (g y) n (l v)", a=PASSES, b=2, g=4, l=FRAMES_LOW
     )
-    for a in range(PASSES):
-        for b in range(2):
-            nc.sync.dma_start(
-                out=raw[b:P:2, a, :, :],
-                in_=runs[head, a, b, :, first_sample : first_sample + GROUP, :],
-            )
+    for b in range(2):
+        nc.sync.dma_start(
+            out=raw[b:P:2, :, :],
+            in_=runs[head, a, b, :, first_sample : first_sample + GROUP, :],
+        )
     return raw
 
 
 def turn(nc, pool, raw):
-    turned = pool.tile([P, WIDTH], BF16, align_bytes=64)
+    turned = pool.tile([P, GROUP * RUN], BF16, align_bytes=64)
     nc.vector.transpose(
-        out=turned[:].bitcast(F32),
-        in_=raw[:].rearrange("p a n e -> p (a n e)").bitcast(F32),
+        out=turned[:].bitcast(F32), in_=raw[:].rearrange("p n e -> p (n e)").bitcast(F32)
     )
     return turned
 
 
-def quantise(nc, pool, turned):
-    codes = pool.tile([P, PASSES, GROUP, FRAMES], U32, align_bytes=64)
-    scales = pool.tile([P, PASSES, GROUP, FRAMES], U8, align_bytes=64)
+def quantise(nc, turned, codes, scales):
     nc.vector.quantize_mx(
-        out=codes[:].rearrange("p a n f -> p (a n f)").bitcast(FP8X4),
-        scales=scales[:].rearrange("p a n f -> p (a n f)"),
+        out=codes.rearrange("p n f -> p (n f)").bitcast(FP8X4),
+        scales=scales.rearrange("p n f -> p (n f)"),
         in_=turned[:],
     )
-    return codes, scales
 
 
 def tile_model_pa_t_kernel(tc, q, k, alphas, att1s, out):
@@ -63,35 +56,43 @@ def tile_model_pa_t_kernel(tc, q, k, alphas, att1s, out):
 
     with ExitStack() as stack:
         const = stack.enter_context(tc.tile_pool(name="const", bufs=1))
-        raw_pool = stack.enter_context(tc.tile_pool(name="raw", bufs=len(rounds)))
-        turned_pool = stack.enter_context(tc.tile_pool(name="turned", bufs=3))
-        mx_pool = stack.enter_context(tc.tile_pool(name="mx", bufs=4))
+        raw_pool = stack.enter_context(tc.tile_pool(name="raw", bufs=len(rounds) * PASSES))
+        turned_pool = stack.enter_context(tc.tile_pool(name="turned", bufs=4))
+        mx_pool = stack.enter_context(tc.tile_pool(name="mx", bufs=2))
         squashed_pool = stack.enter_context(tc.tile_pool(name="squashed", bufs=2))
         result_pool = stack.enter_context(tc.tile_pool(name="result", bufs=LAG))
         scores_pool = stack.enter_context(tc.psum_pool(name="scores", bufs=PSUM_BANKS - LAG))
         by_frame_pool = stack.enter_context(tc.psum_pool(name="by_frame", bufs=LAG))
 
+        stack.enter_context(tc.manual_schedule())
+
         raws = [
-            (load(nc, raw_pool, q, head, first, "q_raw"), load(nc, raw_pool, k, head, first, "k_raw"))
+            [
+                (
+                    load(nc, raw_pool, q, head, first, a, "q_raw"),
+                    load(nc, raw_pool, k, head, first, a, "k_raw"),
+                )
+                for a in range(PASSES)
+            ]
             for head, first in rounds
         ]
 
         static_map = const.tile([P, HEADS, FRAMES], BF16)
-        nc.scalar.dma_start(out=static_map[:], in_=att1s[0].rearrange("h t u -> t h u"))
+        nc.sync.dma_start(out=static_map[:], in_=att1s[0].rearrange("h t u -> t h u"))
         gain_bf = const.tile([P, HEADS], BF16)
-        nc.scalar.dma_start(
+        nc.sync.dma_start(
             out=gain_bf[:], in_=alphas.rearrange("a h b c -> (a h b c)").partition_broadcast(P)
         )
-        gain = const.tile([P, HEADS], F32)
-        nc.vector.tensor_copy(out=gain[:], in_=gain_bf[:])
 
         identity = const.tile([P, P], F32)
         make_identity(nc, identity[:])
         sort_frames = const.tile([P, P], F32)
-        nc.vector.tensor_copy(
+        nc.gpsimd.tensor_copy(
             out=sort_frames[:].rearrange("p (y l) -> p y l", l=FRAMES_LOW),
             in_=identity[:].rearrange("p (l y) -> p y l", l=FRAMES_LOW),
         )
+        gain = const.tile([P, HEADS], F32)
+        nc.gpsimd.tensor_copy(out=gain[:], in_=gain_bf[:])
 
         def finish(head, first, by_frame):
             result = result_pool.tile([P, GROUP, FRAMES], F32)
@@ -107,15 +108,20 @@ def tile_model_pa_t_kernel(tc, q, k, alphas, att1s, out):
                 out=out[first : first + GROUP, head].rearrange("n t u -> t n u"), in_=result[:]
             )
 
-        stack.enter_context(tc.manual_schedule())
         waiting = []
-        for r, ((head, first), (q_raw, k_raw)) in enumerate(zip(rounds, raws)):
-            q_turned = turn(nc, turned_pool, q_raw)
-            k_turned = turn(nc, turned_pool, k_raw)
+        for r, (head, first) in enumerate(rounds):
+            q_codes = mx_pool.tile([P, PASSES, GROUP, FRAMES], U32, align_bytes=64)
+            q_scales = mx_pool.tile([P, PASSES, GROUP, FRAMES], U8, align_bytes=64)
+            k_codes = mx_pool.tile([P, PASSES, GROUP, FRAMES], U32, align_bytes=64)
+            k_scales = mx_pool.tile([P, PASSES, GROUP, FRAMES], U8, align_bytes=64)
+            for a in range(PASSES):
+                q_raw, k_raw = raws[r][a]
+                q_turned = turn(nc, turned_pool, q_raw)
+                k_turned = turn(nc, turned_pool, k_raw)
+                quantise(nc, q_turned, q_codes[:, a], q_scales[:, a])
+                quantise(nc, k_turned, k_codes[:, a], k_scales[:, a])
             if r >= LAG:
                 finish(*waiting[r - LAG])
-            q_codes, q_scales = quantise(nc, mx_pool, q_turned)
-            k_codes, k_scales = quantise(nc, mx_pool, k_turned)
 
             scores = scores_pool.tile([P, GROUP, FRAMES], F32)
             for n in range(GROUP):

@@ -15,138 +15,174 @@ FLOPS = 2 * SAMPLES * HEADS * FRAMES * FRAMES * CHANNELS * JOINTS
 P = 128
 PASSES = CHANNELS * JOINTS // (4 * P)
 GROUP = 4
-FRAMES_LOW = 8
-RUN = FRAMES_LOW * JOINTS
-PSUM_BANKS = 8
-LAG = 7
+CB = 4
+CA = CHANNELS // CB
+Y = P // (CA * GROUP)
+L = FRAMES // Y
+RUN = L * JOINTS
+PER_BANK = 4
+WORDS = JOINTS // 2
+COLS = PASSES * GROUP * Y
 
 
-def load(nc, pool, x, head, first_sample, a, name):
-    raw = pool.tile([P, GROUP, RUN], BF16, name=name, align_bytes=64)
-    runs = x.rearrange(
-        "n h (a b g) (y l) v -> h a b (g y) n (l v)", a=PASSES, b=2, g=4, l=FRAMES_LOW
-    )
-    for b in range(2):
-        nc.sync.dma_start(
-            out=raw[b:P:2, :, :],
-            in_=runs[head, a, b, :, first_sample : first_sample + GROUP, :],
-        )
+def load(nc, pool, x, head, first):
+    raw = pool.tile([P, CB, RUN], BF16, name="raw", align_bytes=64)
+    runs = x.rearrange("n h (cb ca) (y l) v -> h n (ca y) cb (l v)", ca=CA, l=L)
+    for n in range(GROUP):
+        nc.sync.dma_start(out=raw[n:P:GROUP, :, :], in_=runs[head, first + n])
     return raw
-
-
-def turn(nc, pool, raw):
-    turned = pool.tile([P, GROUP * RUN], BF16, align_bytes=64)
-    nc.vector.transpose(
-        out=turned[:].bitcast(F32), in_=raw[:].rearrange("p n e -> p (n e)").bitcast(F32)
-    )
-    return turned
-
-
-def quantise(nc, turned, codes, scales):
-    nc.vector.quantize_mx(
-        out=codes.rearrange("p n f -> p (n f)").bitcast(FP8X4),
-        scales=scales.rearrange("p n f -> p (n f)"),
-        in_=turned[:],
-    )
 
 
 def tile_model_pa_t_kernel(tc, q, k, alphas, att1s, out):
     nc = tc.nc
     rounds = [(head, first) for head in range(HEADS) for first in range(0, SAMPLES, GROUP)]
+    units = [(x, head, first) for head, first in rounds for x in (q, k)]
 
     with ExitStack() as stack:
         const = stack.enter_context(tc.tile_pool(name="const", bufs=1))
-        raw_pool = stack.enter_context(tc.tile_pool(name="raw", bufs=len(rounds) * PASSES))
-        turned_pool = stack.enter_context(tc.tile_pool(name="turned", bufs=4))
-        mx_pool = stack.enter_context(tc.tile_pool(name="mx", bufs=2))
+        raw_pool = stack.enter_context(tc.tile_pool(name="raw", bufs=len(units)))
+        arranged_pool = stack.enter_context(tc.tile_pool(name="arranged", bufs=3))
+        turned_pool = stack.enter_context(tc.tile_pool(name="turned", bufs=3))
+        mx_pool = stack.enter_context(tc.tile_pool(name="mx", bufs=5))
         squashed_pool = stack.enter_context(tc.tile_pool(name="squashed", bufs=2))
-        result_pool = stack.enter_context(tc.tile_pool(name="result", bufs=LAG))
-        scores_pool = stack.enter_context(tc.psum_pool(name="scores", bufs=PSUM_BANKS - LAG))
-        by_frame_pool = stack.enter_context(tc.psum_pool(name="by_frame", bufs=LAG))
+        result_pool = stack.enter_context(tc.tile_pool(name="result", bufs=len(rounds)))
+        scores_pool = stack.enter_context(tc.psum_pool(name="scores", bufs=2))
+        bank_pool = stack.enter_context(tc.psum_pool(name="bank", bufs=6))
 
         stack.enter_context(tc.manual_schedule())
 
-        raws = [
-            [
-                (
-                    load(nc, raw_pool, q, head, first, a, "q_raw"),
-                    load(nc, raw_pool, k, head, first, a, "k_raw"),
-                )
-                for a in range(PASSES)
-            ]
-            for head, first in rounds
-        ]
-
-        static_map = const.tile([P, HEADS, FRAMES], BF16)
-        nc.sync.dma_start(out=static_map[:], in_=att1s[0].rearrange("h t u -> t h u"))
-        gain_bf = const.tile([P, HEADS], BF16)
-        nc.sync.dma_start(
-            out=gain_bf[:], in_=alphas.rearrange("a h b c -> (a h b c)").partition_broadcast(P)
+        warm = const.tile([P, 1], F32)
+        nc.gpsimd.memset(warm[:], 0.0)
+        warmed = const.tile([P, 1], F32)
+        nc.scalar.activation(
+            out=warmed[:], in_=warm[:], func=mybir.ActivationFunctionType.Tanh
         )
+
+        raws = []
+        for u, (x, head, first) in enumerate(units):
+            raws.append(load(nc, raw_pool, x, head, first))
+            if u == 1:
+                static_map = const.tile([P, HEADS, FRAMES], BF16)
+                nc.sync.dma_start(out=static_map[:], in_=att1s[0].rearrange("h t u -> t h u"))
+                gain_bf = const.tile([P, HEADS], BF16)
+                nc.sync.dma_start(
+                    out=gain_bf[:],
+                    in_=alphas.rearrange("a h b c -> (a h b c)").partition_broadcast(P),
+                )
 
         identity = const.tile([P, P], F32)
         make_identity(nc, identity[:])
-        sort_frames = const.tile([P, P], F32)
-        nc.gpsimd.tensor_copy(
-            out=sort_frames[:].rearrange("p (y l) -> p y l", l=FRAMES_LOW),
-            in_=identity[:].rearrange("p (l y) -> p y l", l=FRAMES_LOW),
-        )
+        sort_rows = const.tile([P, P], F32)
+        for a in range(PASSES):
+            nc.gpsimd.tensor_copy(
+                out=sort_rows[:].rearrange("p (a n y g) -> p a n y g", a=PASSES, y=Y, g=2)[:, a],
+                in_=identity[:].rearrange("p (g a y n) -> p a n y g", a=PASSES, y=Y, g=2)[:, a],
+            )
         gain = const.tile([P, HEADS], F32)
         nc.gpsimd.tensor_copy(out=gain[:], in_=gain_bf[:])
 
-        def finish(head, first, by_frame):
-            result = result_pool.tile([P, GROUP, FRAMES], F32)
+        arranged = [None] * len(units)
+        turned = [None] * len(units)
+        codes = [None] * len(units)
+        scales = [None] * len(units)
+        scores = [None] * len(rounds)
+        squashed = [None] * len(rounds)
+
+        def arrange(u):
+            tile = arranged_pool.tile([P, L, CB, JOINTS], BF16, name="arr", align_bytes=64)
+            nc.vector.tensor_copy(
+                out=tile[:], in_=raws[u][:].rearrange("p cb (l v) -> p l cb v", v=JOINTS)
+            )
+            arranged[u] = tile
+
+        def transpose_bank(u, b):
+            if b == 0:
+                turned[u] = turned_pool.tile([P, COLS * L * 4], BF16, name="trn", align_bytes=64)
+            bank = bank_pool.tile([P, PER_BANK, P], F32, name="bank")
+            words = arranged[u][:].rearrange("p l cb v -> p (l cb v)").bitcast(F32)
+            for j in range(PER_BANK):
+                low = (b * PER_BANK + j) * P
+                nc.tensor.transpose(bank[:, j, :], words[:, low : low + P], sort_rows[:])
+            return bank
+
+        def leave_bank(u, b, bank):
+            nc.scalar.copy(
+                out=turned[u][:]
+                .bitcast(F32)
+                .rearrange("p (x l g) -> p x l g", l=L, g=2)[
+                    :, :, b * PER_BANK : (b + 1) * PER_BANK, :
+                ],
+                in_=bank[:].rearrange("p l (x g) -> p x l g", g=2),
+            )
+
+        def quantise(u):
+            codes[u] = mx_pool.tile(
+                [P, PASSES, GROUP, FRAMES], U32, name="codes", align_bytes=64
+            )
+            scales[u] = mx_pool.tile(
+                [P, PASSES, GROUP, FRAMES], U8, name="scales", align_bytes=64
+            )
+            nc.vector.quantize_mx(
+                out=codes[u][:].rearrange("p a n f -> p (a n f)").bitcast(FP8X4),
+                scales=scales[u][:].rearrange("p a n f -> p (a n f)"),
+                in_=turned[u][:],
+            )
+
+        def multiply(r):
+            scores[r] = scores_pool.tile([P, GROUP, FRAMES], F32, name="sc")
+            for n in range(GROUP):
+                for a in range(PASSES):
+                    nc.tensor.matmul_mx(
+                        out=scores[r][:, n, :],
+                        lhsT=codes[2 * r][:, a, n, :].bitcast(FP8X4),
+                        lhsT_scale=scales[2 * r][:, a, n, :],
+                        rhs=codes[2 * r + 1][:, a, n, :].bitcast(FP8X4),
+                        rhs_scale=scales[2 * r + 1][:, a, n, :],
+                        start=(a == 0),
+                        stop=(a == PASSES - 1),
+                    )
+
+        def squash(r):
+            squashed[r] = squashed_pool.tile([P, GROUP, FRAMES], F32, name="sq")
+            nc.scalar.activation(
+                out=squashed[r][:],
+                in_=scores[r][:],
+                func=mybir.ActivationFunctionType.Tanh,
+                scale=1.0 / (CHANNELS * JOINTS),
+            )
+
+        def finish(r):
+            head, first = rounds[r]
+            result = result_pool.tile([P, GROUP, FRAMES], F32, name="res")
             nc.vector.scalar_tensor_tensor(
                 out=result[:],
-                in0=by_frame[:],
+                in0=squashed[r][:],
                 scalar=gain[:, head : head + 1],
                 in1=static_map[:, head, :].unsqueeze(1).to_broadcast([P, GROUP, FRAMES]),
                 op0=mybir.AluOpType.mult,
                 op1=mybir.AluOpType.add,
             )
-            nc.scalar.dma_start(
+            nc.sync.dma_start(
                 out=out[first : first + GROUP, head].rearrange("n t u -> t n u"), in_=result[:]
             )
 
-        waiting = []
-        for r, (head, first) in enumerate(rounds):
-            q_codes = mx_pool.tile([P, PASSES, GROUP, FRAMES], U32, align_bytes=64)
-            q_scales = mx_pool.tile([P, PASSES, GROUP, FRAMES], U8, align_bytes=64)
-            k_codes = mx_pool.tile([P, PASSES, GROUP, FRAMES], U32, align_bytes=64)
-            k_scales = mx_pool.tile([P, PASSES, GROUP, FRAMES], U8, align_bytes=64)
-            for a in range(PASSES):
-                q_raw, k_raw = raws[r][a]
-                q_turned = turn(nc, turned_pool, q_raw)
-                k_turned = turn(nc, turned_pool, k_raw)
-                quantise(nc, q_turned, q_codes[:, a], q_scales[:, a])
-                quantise(nc, k_turned, k_codes[:, a], k_scales[:, a])
-            if r >= LAG:
-                finish(*waiting[r - LAG])
-
-            scores = scores_pool.tile([P, GROUP, FRAMES], F32)
-            for n in range(GROUP):
-                for a in range(PASSES):
-                    nc.tensor.matmul_mx(
-                        out=scores[:, n, :],
-                        lhsT=k_codes[:, a, n, :].bitcast(FP8X4),
-                        lhsT_scale=k_scales[:, a, n, :],
-                        rhs=q_codes[:, a, n, :].bitcast(FP8X4),
-                        rhs_scale=q_scales[:, a, n, :],
-                        start=(a == 0),
-                        stop=(a == PASSES - 1),
-                    )
-
-            squashed = squashed_pool.tile([P, GROUP, FRAMES], F32)
-            nc.scalar.activation(
-                out=squashed[:].rearrange("p n (y l) -> p n y l", l=FRAMES_LOW),
-                in_=scores[:].rearrange("p n (l y) -> p n y l", l=FRAMES_LOW),
-                func=mybir.ActivationFunctionType.Tanh,
-                scale=1.0 / (CHANNELS * JOINTS),
-            )
-
-            by_frame = by_frame_pool.tile([P, GROUP, FRAMES], F32)
-            for n in range(GROUP):
-                nc.tensor.transpose(by_frame[:, n, :], squashed[:, n, :], sort_frames[:])
-            waiting.append((head, first, by_frame))
-        for late in waiting[len(rounds) - LAG :]:
-            finish(*late)
+        last = len(units)
+        arrange(0)
+        for u in range(last + 4):
+            if u + 1 < last:
+                arrange(u + 1)
+            if 0 <= u - 1 < last:
+                quantise(u - 1)
+            if u % 2 == 0 and 0 <= u - 4 < last:
+                finish((u - 4) // 2)
+            r = (u - 3) // 2
+            ready = u % 2 == 1 and 0 <= r < len(rounds)
+            if u < last:
+                for b in range(L // PER_BANK):
+                    leave_bank(u, b, transpose_bank(u, b))
+                    if b == 1 and ready:
+                        multiply(r)
+            elif ready:
+                multiply(r)
+            if ready:
+                squash(r)

@@ -27,9 +27,11 @@ COLS = PASSES * GROUP * Y
 
 def load(nc, pool, x, head, first):
     raw = pool.tile([P, CB, RUN], BF16, name="raw", align_bytes=64)
-    runs = x.rearrange("n h (cb ca) (y l) v -> h n (ca y) cb (l v)", ca=CA, l=L)
-    for n in range(GROUP):
-        nc.sync.dma_start(out=raw[n:P:GROUP, :, :], in_=runs[head, first + n])
+    runs = x.rearrange("n h (cb ca) (y l) v -> h cb (ca y) n (l v)", ca=CA, l=L)
+    for cb in range(CB):
+        nc.sync.dma_start(
+            out=raw[:, cb, :], in_=runs[head, cb, :, first : first + GROUP, :]
+        )
     return raw
 
 

@@ -25,13 +25,15 @@ WORDS = JOINTS // 2
 COLS = PASSES * GROUP * Y
 
 
-def load(nc, pool, x, head, first):
+def load(nc, pool, x, head, first, parts):
     raw = pool.tile([P, CB, RUN], BF16, name="raw", align_bytes=64)
     runs = x.rearrange("n h (cb ca) (y l) v -> h cb (ca y) n (l v)", ca=CA, l=L)
-    for cb in range(CB):
-        nc.sync.dma_start(
-            out=raw[:, cb, :], in_=runs[head, cb, :, first : first + GROUP, :]
-        )
+    for i in range(parts):
+        piece = slice(i * RUN // parts, (i + 1) * RUN // parts)
+        for cb in range(CB):
+            nc.sync.dma_start(
+                out=raw[:, cb, piece], in_=runs[head, cb, :, first : first + GROUP, piece]
+            )
     return raw
 
 
@@ -62,8 +64,8 @@ def tile_model_pa_t_kernel(tc, q, k, alphas, att1s, out):
 
         raws = []
         for u, (x, head, first) in enumerate(units):
-            raws.append(load(nc, raw_pool, x, head, first))
-            if u == 1:
+            raws.append(load(nc, raw_pool, x, head, first, 2 if u in (0, len(units) - 1) else 1))
+            if u == 3:
                 static_map = const.tile([P, HEADS, FRAMES], BF16)
                 nc.sync.dma_start(out=static_map[:], in_=att1s[0].rearrange("h t u -> t h u"))
                 gain_bf = const.tile([P, HEADS], BF16)
@@ -77,7 +79,7 @@ def tile_model_pa_t_kernel(tc, q, k, alphas, att1s, out):
         sort_rows = const.tile([P, P], F32)
         for a in range(PASSES):
             nc.gpsimd.tensor_copy(
-                out=sort_rows[:].rearrange("p (a n y g) -> p a n y g", a=PASSES, y=Y, g=2)[:, a],
+                out=sort_rows[:].rearrange("p (n a y g) -> p a n y g", a=PASSES, y=Y, g=2)[:, a],
                 in_=identity[:].rearrange("p (g a y n) -> p a n y g", a=PASSES, y=Y, g=2)[:, a],
             )
         gain = const.tile([P, HEADS], F32)
@@ -89,12 +91,14 @@ def tile_model_pa_t_kernel(tc, q, k, alphas, att1s, out):
         scales = [None] * len(units)
         scores = [None] * len(rounds)
         squashed = [None] * len(rounds)
+        results = [None] * len(rounds)
 
-        def arrange(u):
+        def arrange(u, parts=1):
             tile = arranged_pool.tile([P, L, CB, JOINTS], BF16, name="arr", align_bytes=64)
-            nc.vector.tensor_copy(
-                out=tile[:], in_=raws[u][:].rearrange("p cb (l v) -> p l cb v", v=JOINTS)
-            )
+            frames = raws[u][:].rearrange("p cb (l v) -> p l cb v", v=JOINTS)
+            for i in range(parts):
+                piece = slice(i * L // parts, (i + 1) * L // parts)
+                nc.vector.tensor_copy(out=tile[:, piece], in_=frames[:, piece])
             arranged[u] = tile
 
         def transpose_bank(u, b):
@@ -107,8 +111,8 @@ def tile_model_pa_t_kernel(tc, q, k, alphas, att1s, out):
                 nc.tensor.transpose(bank[:, j, :], words[:, low : low + P], sort_rows[:])
             return bank
 
-        def leave_bank(u, b, bank):
-            nc.scalar.copy(
+        def leave_bank(u, b, bank, copy):
+            copy(
                 out=turned[u][:]
                 .bitcast(F32)
                 .rearrange("p (x l g) -> p x l g", l=L, g=2)[
@@ -117,74 +121,98 @@ def tile_model_pa_t_kernel(tc, q, k, alphas, att1s, out):
                 in_=bank[:].rearrange("p l (x g) -> p x l g", g=2),
             )
 
-        def quantise(u):
+        def quantise(u, parts=1):
             codes[u] = mx_pool.tile(
-                [P, PASSES, GROUP, FRAMES], U32, name="codes", align_bytes=64
+                [P, GROUP, PASSES, FRAMES], U32, name="codes", align_bytes=64
             )
             scales[u] = mx_pool.tile(
-                [P, PASSES, GROUP, FRAMES], U8, name="scales", align_bytes=64
+                [P, GROUP, PASSES, FRAMES], U8, name="scales", align_bytes=64
             )
-            nc.vector.quantize_mx(
-                out=codes[u][:].rearrange("p a n f -> p (a n f)").bitcast(FP8X4),
-                scales=scales[u][:].rearrange("p a n f -> p (a n f)"),
-                in_=turned[u][:],
-            )
+            for i in range(parts):
+                some = slice(i * GROUP // parts, (i + 1) * GROUP // parts)
+                size = GROUP * PASSES * FRAMES * 4 // parts
+                nc.vector.quantize_mx(
+                    out=codes[u][:, some].rearrange("p n a f -> p (n a f)").bitcast(FP8X4),
+                    scales=scales[u][:, some].rearrange("p n a f -> p (n a f)"),
+                    in_=turned[u][:, i * size : (i + 1) * size],
+                )
 
-        def multiply(r):
-            scores[r] = scores_pool.tile([P, GROUP, FRAMES], F32, name="sc")
-            for n in range(GROUP):
+        def multiply(r, some=slice(0, GROUP)):
+            if some.start == 0:
+                scores[r] = scores_pool.tile([P, GROUP, FRAMES], F32, name="sc")
+            for n in range(some.start, some.stop):
                 for a in range(PASSES):
                     nc.tensor.matmul_mx(
                         out=scores[r][:, n, :],
-                        lhsT=codes[2 * r][:, a, n, :].bitcast(FP8X4),
-                        lhsT_scale=scales[2 * r][:, a, n, :],
-                        rhs=codes[2 * r + 1][:, a, n, :].bitcast(FP8X4),
-                        rhs_scale=scales[2 * r + 1][:, a, n, :],
+                        lhsT=codes[2 * r][:, n, a, :].bitcast(FP8X4),
+                        lhsT_scale=scales[2 * r][:, n, a, :],
+                        rhs=codes[2 * r + 1][:, n, a, :].bitcast(FP8X4),
+                        rhs_scale=scales[2 * r + 1][:, n, a, :],
                         start=(a == 0),
                         stop=(a == PASSES - 1),
                     )
 
-        def squash(r):
-            squashed[r] = squashed_pool.tile([P, GROUP, FRAMES], F32, name="sq")
+        def squash(r, some=slice(0, GROUP)):
+            if some.start == 0:
+                squashed[r] = squashed_pool.tile([P, GROUP, FRAMES], F32, name="sq")
             nc.scalar.activation(
-                out=squashed[r][:],
-                in_=scores[r][:],
+                out=squashed[r][:, some],
+                in_=scores[r][:, some],
                 func=mybir.ActivationFunctionType.Tanh,
                 scale=1.0 / (CHANNELS * JOINTS),
             )
 
-        def finish(r):
+        def finish(r, some=slice(0, GROUP)):
             head, first = rounds[r]
-            result = result_pool.tile([P, GROUP, FRAMES], F32, name="res")
+            if some.start == 0:
+                results[r] = result_pool.tile([P, GROUP, FRAMES], F32, name="res")
+            count = some.stop - some.start
             nc.vector.scalar_tensor_tensor(
-                out=result[:],
-                in0=squashed[r][:],
+                out=results[r][:, some],
+                in0=squashed[r][:, some],
                 scalar=gain[:, head : head + 1],
-                in1=static_map[:, head, :].unsqueeze(1).to_broadcast([P, GROUP, FRAMES]),
+                in1=static_map[:, head, :].unsqueeze(1).to_broadcast([P, count, FRAMES]),
                 op0=mybir.AluOpType.mult,
                 op1=mybir.AluOpType.add,
             )
             nc.sync.dma_start(
-                out=out[first : first + GROUP, head].rearrange("n t u -> t n u"), in_=result[:]
+                out=out[first + some.start : first + some.stop, head].rearrange("n t u -> t n u"),
+                in_=results[r][:, some],
             )
 
-        last = len(units)
-        arrange(0)
-        for u in range(last + 4):
-            if u + 1 < last:
-                arrange(u + 1)
-            if 0 <= u - 1 < last:
+        last = len(units) - 1
+        banks = L // PER_BANK
+        arrange(0, 2)
+        for u in range(last):
+            if 1 <= u <= 3:
                 quantise(u - 1)
-            if u % 2 == 0 and 0 <= u - 4 < last:
+            arrange(u + 1, 2 if u + 1 == last else 1)
+            if u > 3:
+                quantise(u - 1)
+            if u % 2 == 0 and u >= 4:
                 finish((u - 4) // 2)
-            r = (u - 3) // 2
-            ready = u % 2 == 1 and 0 <= r < len(rounds)
-            if u < last:
-                for b in range(L // PER_BANK):
-                    leave_bank(u, b, transpose_bank(u, b))
-                    if b == 1 and ready:
-                        multiply(r)
-            elif ready:
-                multiply(r)
+            ready = u % 2 == 1 and u >= 3
+            for b in range(banks):
+                leave_bank(u, b, transpose_bank(u, b), nc.scalar.copy)
+                if b == 1 and ready:
+                    multiply((u - 3) // 2)
             if ready:
-                squash(r)
+                squash((u - 3) // 2)
+
+        r = len(rounds) - 1
+        quantise(last - 1)
+        for b in range(banks):
+            leave_bank(
+                last,
+                b,
+                transpose_bank(last, b),
+                nc.scalar.copy if b < banks - 1 else nc.vector.tensor_copy,
+            )
+        multiply(r - 1)
+        squash(r - 1)
+        quantise(last, 2)
+        finish(r - 1)
+        for some in (slice(0, GROUP // 2), slice(GROUP // 2, GROUP)):
+            multiply(r, some)
+            squash(r, some)
+            finish(r, some)

@@ -20,6 +20,7 @@ CA = CHANNELS // CB
 Y = P // (CA * GROUP)
 L = FRAMES // Y
 RUN = L * JOINTS
+BUSY_PASSES = 2
 PER_BANK = 4
 WORDS = JOINTS // 2
 COLS = PASSES * GROUP * Y
@@ -137,8 +138,22 @@ def tile_model_pa_t_kernel(tc, q, k, alphas, att1s, out):
                     in_=turned[u][:, i * size : (i + 1) * size],
                 )
 
+        def keep_busy(r):
+            scores[r] = scores_pool.tile([P, GROUP, FRAMES], F32, name="sc")
+            wide = slice(0, GROUP // PASSES)
+            for i in range(BUSY_PASSES):
+                nc.tensor.matmul_mx(
+                    out=scores[r][:].rearrange("p n u -> p (n u)"),
+                    lhsT=codes[2 * r][:, 0, 0, :].bitcast(FP8X4),
+                    lhsT_scale=scales[2 * r][:, 0, 0, :],
+                    rhs=codes[2 * r][:, wide].rearrange("p n a f -> p (n a f)").bitcast(FP8X4),
+                    rhs_scale=scales[2 * r][:, wide].rearrange("p n a f -> p (n a f)"),
+                    start=True,
+                    stop=True,
+                )
+
         def multiply(r, some=slice(0, GROUP)):
-            if some.start == 0:
+            if scores[r] is None:
                 scores[r] = scores_pool.tile([P, GROUP, FRAMES], F32, name="sc")
             for n in range(some.start, some.stop):
                 for a in range(PASSES):
@@ -196,6 +211,8 @@ def tile_model_pa_t_kernel(tc, q, k, alphas, att1s, out):
                 leave_bank(u, b, transpose_bank(u, b), nc.scalar.copy)
                 if b == 1 and ready:
                     multiply((u - 3) // 2)
+                if b == 1 and u % 2 == 0 and u >= 2:
+                    keep_busy((u - 2) // 2)
             if ready:
                 squash((u - 3) // 2)
 

@@ -20,6 +20,7 @@ CA = CHANNELS // CB
 Y = P // (CA * GROUP)
 L = FRAMES // Y
 RUN = L * JOINTS
+SPLIT = (0, 1, 2 * HEADS * SAMPLES // GROUP - 1)
 BUSY_PASSES = 2
 PER_BANK = 4
 WORDS = JOINTS // 2
@@ -50,7 +51,7 @@ def tile_model_pa_t_kernel(tc, q, k, alphas, att1s, out):
         turned_pool = stack.enter_context(tc.tile_pool(name="turned", bufs=3))
         mx_pool = stack.enter_context(tc.tile_pool(name="mx", bufs=5))
         squashed_pool = stack.enter_context(tc.tile_pool(name="squashed", bufs=2))
-        result_pool = stack.enter_context(tc.tile_pool(name="result", bufs=len(rounds)))
+        result_pool = stack.enter_context(tc.tile_pool(name="result", bufs=HEADS + 2))
         scores_pool = stack.enter_context(tc.psum_pool(name="scores", bufs=2))
         bank_pool = stack.enter_context(tc.psum_pool(name="bank", bufs=6))
 
@@ -65,8 +66,8 @@ def tile_model_pa_t_kernel(tc, q, k, alphas, att1s, out):
 
         raws = []
         for u, (x, head, first) in enumerate(units):
-            raws.append(load(nc, raw_pool, x, head, first, 2 if u in (0, len(units) - 1) else 1))
-            if u == 3:
+            raws.append(load(nc, raw_pool, x, head, first, 2 if u in SPLIT else 1))
+            if u == 6:
                 static_map = const.tile([P, HEADS, FRAMES], BF16)
                 nc.sync.dma_start(out=static_map[:], in_=att1s[0].rearrange("h t u -> t h u"))
                 gain_bf = const.tile([P, HEADS], BF16)
@@ -92,7 +93,6 @@ def tile_model_pa_t_kernel(tc, q, k, alphas, att1s, out):
         scales = [None] * len(units)
         scores = [None] * len(rounds)
         squashed = [None] * len(rounds)
-        results = [None] * len(rounds)
 
         def arrange(u, parts=1):
             tile = arranged_pool.tile([P, L, CB, JOINTS], BF16, name="arr", align_bytes=64)
@@ -112,14 +112,16 @@ def tile_model_pa_t_kernel(tc, q, k, alphas, att1s, out):
                 nc.tensor.transpose(bank[:, j, :], words[:, low : low + P], sort_rows[:])
             return bank
 
-        def leave_bank(u, b, bank, copy):
+        def leave_bank(u, b, bank, copy, some=slice(0, GROUP)):
+            size = COLS // GROUP
+            piece = slice(some.start * size, some.stop * size)
             copy(
                 out=turned[u][:]
                 .bitcast(F32)
                 .rearrange("p (x l g) -> p x l g", l=L, g=2)[
-                    :, :, b * PER_BANK : (b + 1) * PER_BANK, :
+                    :, piece, b * PER_BANK : (b + 1) * PER_BANK, :
                 ],
-                in_=bank[:].rearrange("p l (x g) -> p x l g", g=2),
+                in_=bank[:].rearrange("p l (x g) -> p x l g", g=2)[:, piece],
             )
 
         def quantise(u, parts=1):
@@ -154,11 +156,11 @@ def tile_model_pa_t_kernel(tc, q, k, alphas, att1s, out):
 
         def multiply(r, some=slice(0, GROUP)):
             if scores[r] is None:
-                scores[r] = scores_pool.tile([P, GROUP, FRAMES], F32, name="sc")
+                scores[r] = scores_pool.tile([P, some.stop - some.start, FRAMES], F32, name="sc")
             for n in range(some.start, some.stop):
                 for a in range(PASSES):
                     nc.tensor.matmul_mx(
-                        out=scores[r][:, n, :],
+                        out=scores[r][:, n - some.start, :],
                         lhsT=codes[2 * r][:, n, a, :].bitcast(FP8X4),
                         lhsT_scale=scales[2 * r][:, n, a, :],
                         rhs=codes[2 * r + 1][:, n, a, :].bitcast(FP8X4),
@@ -168,44 +170,42 @@ def tile_model_pa_t_kernel(tc, q, k, alphas, att1s, out):
                     )
 
         def squash(r, some=slice(0, GROUP)):
-            if some.start == 0:
-                squashed[r] = squashed_pool.tile([P, GROUP, FRAMES], F32, name="sq")
+            head, first = rounds[r]
+            if first == 0:
+                squashed[head] = squashed_pool.tile([P, SAMPLES, FRAMES], F32, name="sq")
             nc.scalar.activation(
-                out=squashed[r][:, some],
-                in_=scores[r][:, some],
+                out=squashed[head][:, first + some.start : first + some.stop],
+                in_=scores[r][:],
                 func=mybir.ActivationFunctionType.Tanh,
                 scale=1.0 / (CHANNELS * JOINTS),
             )
+            scores[r] = None
 
-        def finish(r, some=slice(0, GROUP)):
-            head, first = rounds[r]
-            if some.start == 0:
-                results[r] = result_pool.tile([P, GROUP, FRAMES], F32, name="res")
-            count = some.stop - some.start
+        def finish(head, low, high):
+            result = result_pool.tile([P, high - low, FRAMES], F32, name="res")
             nc.vector.scalar_tensor_tensor(
-                out=results[r][:, some],
-                in0=squashed[r][:, some],
+                out=result[:],
+                in0=squashed[head][:, low:high],
                 scalar=gain[:, head : head + 1],
-                in1=static_map[:, head, :].unsqueeze(1).to_broadcast([P, count, FRAMES]),
+                in1=static_map[:, head, :].unsqueeze(1).to_broadcast([P, high - low, FRAMES]),
                 op0=mybir.AluOpType.mult,
                 op1=mybir.AluOpType.add,
             )
             nc.sync.dma_start(
-                out=out[first + some.start : first + some.stop, head].rearrange("n t u -> t n u"),
-                in_=results[r][:, some],
+                out=out[low:high, head].rearrange("n t u -> t n u"), in_=result[:]
             )
 
         last = len(units) - 1
         banks = L // PER_BANK
         arrange(0, 2)
         for u in range(last):
-            if 1 <= u <= 3:
+            if 1 <= u <= 2:
                 quantise(u - 1)
-            arrange(u + 1, 2 if u + 1 == last else 1)
-            if u > 3:
+            arrange(u + 1, 2 if u == 1 or u + 1 in SPLIT else 1)
+            if u > 2:
                 quantise(u - 1)
-            if u % 2 == 0 and u >= 4:
-                finish((u - 4) // 2)
+            if u % 4 == 2 and u >= 6:
+                finish(u // 4 - 1, 0, SAMPLES)
             ready = u % 2 == 1 and u >= 3
             for b in range(banks):
                 leave_bank(u, b, transpose_bank(u, b), nc.scalar.copy)
@@ -217,19 +217,17 @@ def tile_model_pa_t_kernel(tc, q, k, alphas, att1s, out):
                 squash((u - 3) // 2)
 
         r = len(rounds) - 1
+        halves = (slice(0, GROUP // 2), slice(GROUP // 2, GROUP))
         quantise(last - 1)
-        for b in range(banks):
-            leave_bank(
-                last,
-                b,
-                transpose_bank(last, b),
-                nc.scalar.copy if b < banks - 1 else nc.vector.tensor_copy,
-            )
+        held = [transpose_bank(last, b) for b in range(banks)]
         multiply(r - 1)
+        for some in halves:
+            for b in range(banks):
+                leave_bank(last, b, held[b], nc.scalar.copy, some)
         squash(r - 1)
         quantise(last, 2)
-        finish(r - 1)
-        for some in (slice(0, GROUP // 2), slice(GROUP // 2, GROUP)):
+        finish(HEADS - 1, 0, GROUP)
+        for some in halves:
             multiply(r, some)
             squash(r, some)
-            finish(r, some)
+            finish(HEADS - 1, GROUP + some.start, GROUP + some.stop)

@@ -20,7 +20,8 @@ CA = CHANNELS // CB
 Y = P // (CA * GROUP)
 L = FRAMES // Y
 RUN = L * JOINTS
-SPLIT = (0, 1, 2 * HEADS * SAMPLES // GROUP - 1)
+SPLIT = (0, 2 * HEADS * SAMPLES // GROUP - 1)
+WARM_MATMULS = 6
 BUSY_PASSES = 2
 PER_BANK = 4
 WORDS = JOINTS // 2
@@ -64,6 +65,12 @@ def tile_model_pa_t_kernel(tc, q, k, alphas, att1s, out):
             out=warmed[:], in_=warm[:], func=mybir.ActivationFunctionType.Tanh
         )
 
+        zeros = const.tile([P, PER_BANK * P], BF16)
+        nc.gpsimd.memset(zeros[:], 0.0)
+        unread = bank_pool.tile([P, PER_BANK * P], F32, name="bank")
+        for i in range(WARM_MATMULS):
+            nc.tensor.matmul(unread[:], lhsT=zeros[:, :P], rhs=zeros[:], start=True, stop=True)
+
         raws = []
         for u, (x, head, first) in enumerate(units):
             raws.append(load(nc, raw_pool, x, head, first, 2 if u in SPLIT else 1))
@@ -94,13 +101,16 @@ def tile_model_pa_t_kernel(tc, q, k, alphas, att1s, out):
         scores = [None] * len(rounds)
         squashed = [None] * len(rounds)
 
-        def arrange(u, parts=1):
-            tile = arranged_pool.tile([P, L, CB, JOINTS], BF16, name="arr", align_bytes=64)
-            frames = raws[u][:].rearrange("p cb (l v) -> p l cb v", v=JOINTS)
-            for i in range(parts):
-                piece = slice(i * L // parts, (i + 1) * L // parts)
-                nc.vector.tensor_copy(out=tile[:, piece], in_=frames[:, piece])
-            arranged[u] = tile
+        def arrange(u, part=0, parts=1):
+            if part == 0:
+                arranged[u] = arranged_pool.tile(
+                    [P, L, CB, JOINTS], BF16, name="arr", align_bytes=64
+                )
+            piece = slice(part * L // parts, (part + 1) * L // parts)
+            nc.vector.tensor_copy(
+                out=arranged[u][:, piece],
+                in_=raws[u][:].rearrange("p cb (l v) -> p l cb v", v=JOINTS)[:, piece],
+            )
 
         def transpose_bank(u, b):
             if b == 0:
@@ -197,13 +207,30 @@ def tile_model_pa_t_kernel(tc, q, k, alphas, att1s, out):
 
         last = len(units) - 1
         banks = L // PER_BANK
-        arrange(0, 2)
-        for u in range(last):
+        arrange(0, 0, 2)
+        arrange(0, 1, 2)
+        for b in range(banks):
+            leave_bank(
+                0,
+                b,
+                transpose_bank(0, b),
+                nc.scalar.copy if b < banks - 1 else nc.vector.tensor_copy,
+            )
+        arrange(1, 0, 2)
+        arrange(1, 1, 2)
+        for u in range(1, last):
             if 1 <= u <= 2:
                 quantise(u - 1)
-            arrange(u + 1, 2 if u == 1 or u + 1 in SPLIT else 1)
-            if u > 2:
+            if u <= 2:
+                arrange(u + 1, 0, 2)
+                arrange(u + 1, 1, 2)
+            elif u + 1 < last:
+                arrange(u + 1)
                 quantise(u - 1)
+            else:
+                arrange(last, 0, 2)
+                quantise(last - 2)
+                arrange(last, 1, 2)
             if u % 4 == 2 and u >= 6:
                 finish(u // 4 - 1, 0, SAMPLES)
             ready = u % 2 == 1 and u >= 3

from contextlib import ExitStack

import concourse.mybir as mybir
from concourse.masks import make_identity

F32 = mybir.dt.float32
BF16 = mybir.dt.bfloat16
U32 = mybir.dt.uint32
U8 = mybir.dt.uint8
FP8X4 = mybir.dt.float8_e4m3fn_x4

SAMPLES, HEADS, CHANNELS, FRAMES, JOINTS = 8, 4, 16, 128, 64
FLOPS = 2 * SAMPLES * HEADS * FRAMES * FRAMES * CHANNELS * JOINTS

P = 128
PASSES = CHANNELS * JOINTS // (4 * P)
GROUP = 4
CB = 4
CA = CHANNELS // CB
Y = P // (CA * GROUP)
L = FRAMES // Y
RUN = L * JOINTS
SPLIT = (0, 2 * HEADS * SAMPLES // GROUP - 1)
WARM_MATMULS = 6
BUSY_PASSES = 2
PER_BANK = 4
WORDS = JOINTS // 2
COLS = PASSES * GROUP * Y


def load(nc, pool, x, head, first, parts):
    raw = pool.tile([P, CB, RUN], BF16, name="raw", align_bytes=64)
    runs = x.rearrange("n h (cb ca) (y l) v -> h cb (ca y) n (l v)", ca=CA, l=L)
    for i in range(parts):
        piece = slice(i * RUN // parts, (i + 1) * RUN // parts)
        for cb in range(CB):
            nc.sync.dma_start(
                out=raw[:, cb, piece], in_=runs[head, cb, :, first : first + GROUP, piece]
            )
    return raw


def tile_model_pa_t_kernel(tc, q, k, alphas, att1s, out):
    nc = tc.nc
    rounds = [(head, first) for head in range(HEADS) for first in range(0, SAMPLES, GROUP)]
    units = [(x, head, first) for head, first in rounds for x in (q, k)]

    with ExitStack() as stack:
        const = stack.enter_context(tc.tile_pool(name="const", bufs=1))
        raw_pool = stack.enter_context(tc.tile_pool(name="raw", bufs=len(units)))
        arranged_pool = stack.enter_context(tc.tile_pool(name="arranged", bufs=3))
        turned_pool = stack.enter_context(tc.tile_pool(name="turned", bufs=3))
        mx_pool = stack.enter_context(tc.tile_pool(name="mx", bufs=5))
        squashed_pool = stack.enter_context(tc.tile_pool(name="squashed", bufs=2))
        result_pool = stack.enter_context(tc.tile_pool(name="result", bufs=HEADS + 2))
        scores_pool = stack.enter_context(tc.psum_pool(name="scores", bufs=2))
        bank_pool = stack.enter_context(tc.psum_pool(name="bank", bufs=6))

        stack.enter_context(tc.manual_schedule())

        warm = const.tile([P, 1], F32)
        nc.gpsimd.memset(warm[:], 0.0)
        warmed = const.tile([P, 1], F32)
        nc.scalar.activation(
            out=warmed[:], in_=warm[:], func=mybir.ActivationFunctionType.Tanh
        )

        zeros = const.tile([P, PER_BANK * P], BF16)
        nc.gpsimd.memset(zeros[:], 0.0)
        unread = bank_pool.tile([P, PER_BANK * P], F32, name="bank")
        for i in range(WARM_MATMULS):
            nc.tensor.matmul(unread[:], lhsT=zeros[:, :P], rhs=zeros[:], start=True, stop=True)

        raws = []
        for u, (x, head, first) in enumerate(units):
            raws.append(load(nc, raw_pool, x, head, first, 2 if u in SPLIT else 1))
            if u == 6:
                static_map = const.tile([P, HEADS, FRAMES], BF16)
                nc.sync.dma_start(out=static_map[:], in_=att1s[0].rearrange("h t u -> t h u"))
                gain_bf = const.tile([P, HEADS], BF16)
                nc.sync.dma_start(
                    out=gain_bf[:],
                    in_=alphas.rearrange("a h b c -> (a h b c)").partition_broadcast(P),
                )

        identity = const.tile([P, P], F32)
        make_identity(nc, identity[:])
        sort_rows = const.tile([P, P], F32)
        for a in range(PASSES):
            nc.gpsimd.tensor_copy(
                out=sort_rows[:].rearrange("p (n a y g) -> p a n y g", a=PASSES, y=Y, g=2)[:, a],
                in_=identity[:].rearrange("p (g a y n) -> p a n y g", a=PASSES, y=Y, g=2)[:, a],
            )
        gain = const.tile([P, HEADS], F32)
        nc.gpsimd.tensor_copy(out=gain[:], in_=gain_bf[:])

        arranged = [None] * len(units)
        turned = [None] * len(units)
        codes = [None] * len(units)
        scales = [None] * len(units)
        scores = [None] * len(rounds)
        squashed = [None] * len(rounds)

        def arrange(u, part=0, parts=1):
            if part == 0:
                arranged[u] = arranged_pool.tile(
                    [P, L, CB, JOINTS], BF16, name="arr", align_bytes=64
                )
            piece = slice(part * L // parts, (part + 1) * L // parts)
            nc.vector.tensor_copy(
                out=arranged[u][:, piece],
                in_=raws[u][:].rearrange("p cb (l v) -> p l cb v", v=JOINTS)[:, piece],
            )

        def transpose_bank(u, b):
            if b == 0:
                turned[u] = turned_pool.tile([P, COLS * L * 4], BF16, name="trn", align_bytes=64)
            bank = bank_pool.tile([P, PER_BANK, P], F32, name="bank")
            words = arranged[u][:].rearrange("p l cb v -> p (l cb v)").bitcast(F32)
            for j in range(PER_BANK):
                low = (b * PER_BANK + j) * P
                nc.tensor.transpose(bank[:, j, :], words[:, low : low + P], sort_rows[:])
            return bank

        def leave_bank(u, b, bank, copy, some=slice(0, GROUP)):
            size = COLS // GROUP
            piece = slice(some.start * size, some.stop * size)
            copy(
                out=turned[u][:]
                .bitcast(F32)
                .rearrange("p (x l g) -> p x l g", l=L, g=2)[
                    :, piece, b * PER_BANK : (b + 1) * PER_BANK, :
                ],
                in_=bank[:].rearrange("p l (x g) -> p x l g", g=2)[:, piece],
            )

        def quantise(u, parts=1):
            codes[u] = mx_pool.tile(
                [P, GROUP, PASSES, FRAMES], U32, name="codes", align_bytes=64
            )
            scales[u] = mx_pool.tile(
                [P, GROUP, PASSES, FRAMES], U8, name="scales", align_bytes=64
            )
            for i in range(parts):
                some = slice(i * GROUP // parts, (i + 1) * GROUP // parts)
                size = GROUP * PASSES * FRAMES * 4 // parts
                nc.vector.quantize_mx(
                    out=codes[u][:, some].rearrange("p n a f -> p (n a f)").bitcast(FP8X4),
                    scales=scales[u][:, some].rearrange("p n a f -> p (n a f)"),
                    in_=turned[u][:, i * size : (i + 1) * size],
                )

        def keep_busy(r):
            scores[r] = scores_pool.tile([P, GROUP, FRAMES], F32, name="sc")
            wide = slice(0, GROUP // PASSES)
            for i in range(BUSY_PASSES):
                nc.tensor.matmul_mx(
                    out=scores[r][:].rearrange("p n u -> p (n u)"),
                    lhsT=codes[2 * r][:, 0, 0, :].bitcast(FP8X4),
                    lhsT_scale=scales[2 * r][:, 0, 0, :],
                    rhs=codes[2 * r][:, wide].rearrange("p n a f -> p (n a f)").bitcast(FP8X4),
                    rhs_scale=scales[2 * r][:, wide].rearrange("p n a f -> p (n a f)"),
                    start=True,
                    stop=True,
                )

        def multiply(r, some=slice(0, GROUP)):
            if scores[r] is None:
                scores[r] = scores_pool.tile([P, some.stop - some.start, FRAMES], F32, name="sc")
            for n in range(some.start, some.stop):
                for a in range(PASSES):
                    nc.tensor.matmul_mx(
                        out=scores[r][:, n - some.start, :],
                        lhsT=codes[2 * r][:, n, a, :].bitcast(FP8X4),
                        lhsT_scale=scales[2 * r][:, n, a, :],
                        rhs=codes[2 * r + 1][:, n, a, :].bitcast(FP8X4),
                        rhs_scale=scales[2 * r + 1][:, n, a, :],
                        start=(a == 0),
                        stop=(a == PASSES - 1),
                    )

        def squash(r, some=slice(0, GROUP)):
            head, first = rounds[r]
            if first == 0:
                squashed[head] = squashed_pool.tile([P, SAMPLES, FRAMES], F32, name="sq")
            nc.scalar.activation(
                out=squashed[head][:, first + some.start : first + some.stop],
                in_=scores[r][:],
                func=mybir.ActivationFunctionType.Tanh,
                scale=1.0 / (CHANNELS * JOINTS),
            )
            scores[r] = None

        def finish(head, low, high):
            result = result_pool.tile([P, high - low, FRAMES], F32, name="res")
            nc.vector.scalar_tensor_tensor(
                out=result[:],
                in0=squashed[head][:, low:high],
                scalar=gain[:, head : head + 1],
                in1=static_map[:, head, :].unsqueeze(1).to_broadcast([P, high - low, FRAMES]),
                op0=mybir.AluOpType.mult,
                op1=mybir.AluOpType.add,
            )
            nc.sync.dma_start(
                out=out[low:high, head].rearrange("n t u -> t n u"), in_=result[:]
            )

        last = len(units) - 1
        banks = L // PER_BANK
        arrange(0, 0, 2)
        arrange(0, 1, 2)
        for b in range(banks):
            leave_bank(
                0,
                b,
                transpose_bank(0, b),
                nc.scalar.copy if b < banks - 1 else nc.vector.tensor_copy,
            )
        arrange(1, 0, 2)
        arrange(1, 1, 2)
        for u in range(1, last):
            if 1 <= u <= 2:
                quantise(u - 1)
            if u <= 2:
                arrange(u + 1, 0, 2)
                arrange(u + 1, 1, 2)
            elif u + 1 < last:
                arrange(u + 1)
                quantise(u - 1)
            else:
                arrange(last, 0, 2)
                quantise(last - 2)
                arrange(last, 1, 2)
            if u % 4 == 2 and u >= 6:
                finish(u // 4 - 1, 0, SAMPLES)
            ready = u % 2 == 1 and u >= 3
            for b in range(banks):
                leave_bank(u, b, transpose_bank(u, b), nc.scalar.copy)
                if b == 1 and ready:
                    multiply((u - 3) // 2)
                if b == 1 and u % 2 == 0 and u >= 2:
                    keep_busy((u - 2) // 2)
            if ready:
                squash((u - 3) // 2)

        r = len(rounds) - 1
        halves = (slice(0, GROUP // 2), slice(GROUP // 2, GROUP))
        quantise(last - 1)
        held = [transpose_bank(last, b) for b in range(banks)]
        multiply(r - 1)
        for some in halves:
            for b in range(banks):
                leave_bank(last, b, held[b], nc.scalar.copy, some)
        squash(r - 1)
        quantise(last, 2)
        finish(HEADS - 1, 0, GROUP)
        for some in halves:
            multiply(r, some)
            squash(r, some)
            finish(HEADS - 1, GROUP + some.start, GROUP + some.stop)
